import numpy as np
import ml_dtypes

BF16 = ml_dtypes.bfloat16


def bf(x):
    return np.asarray(x, np.float32).astype(BF16)


def f32(x):
    return np.asarray(x, np.float32)


def f64(x):
    return np.asarray(x).astype(np.float64)


def striped(idx):
    return np.tile(idx.reshape(-1, 16).T, (8, 1))


S, K, M, N, P, Q = 4096, 128, 256, 2048, 3, 1
NV = P + Q
DB = 1 << NV
G, H = K // DB, M // K


def blade_product(a_idx, b_idx):
    metric = [1.0] * P + [-1.0] * Q
    res = [i for i in range(NV) if (a_idx >> i) & 1]
    sign = 1.0
    for b in [i for i in range(NV) if (b_idx >> i) & 1]:
        if b in res:
            sign *= (-1.0) ** (len(res) - res.index(b) - 1)
            sign *= metric[b]
            res.remove(b)
        else:
            res.append(b)
    for i in range(len(res)):
        for j in range(len(res) - i - 1):
            if res[j] > res[j + 1]:
                res[j], res[j + 1] = res[j + 1], res[j]
                sign = -sign
    return sign, sum(1 << bit for bit in res)


def build_cayley():
    cay = np.zeros((DB, DB, DB), np.float32)
    for a in range(DB):
        for b in range(DB):
            s, c = blade_product(a, b)
            cay[a, b, c] = s
    return cay


CAY = build_cayley()


def setup_inputs():
    table = bf(np.random.standard_normal((S, K)))
    mv = f32(bf(np.random.standard_normal((H, G, DB)) / np.sqrt(DB)))
    w = np.zeros((K, M), np.float32)
    for h in range(H):
        for g in range(G):
            w[g * DB:(g + 1) * DB, h * K + g * DB:h * K + (g + 1) * DB] = np.einsum('ijc,j->ic', CAY, mv[h, g])
    return {"table": table, "w": bf(w), "offs": striped(np.random.permutation(S)[:N])}


def reference(table, w, offs):
    idx = offs[:16].T.reshape(-1)
    return f64(w).T @ f64(table)[idx].T

@@ -1,0 +1,61 @@
+import concourse.mybir as mybir
+from concourse.masks import make_identity
+
+BF16, F32, U16 = mybir.dt.bfloat16, mybir.dt.float32, mybir.dt.uint16
+
+P = 128
+S = 4096
+M = 256
+N = 2048
+PIECE = 512
+BLOCKS = 8
+CHUNK = BLOCKS * P
+
+FLOPS = 2 * P * M * N
+
+
+def tile_cliffordalgebra_kernel(tc, table, w, offs, out):
+    nc = tc.nc
+    with (
+        tc.tile_pool(name="held", bufs=1) as held,
+        tc.tile_pool(name="staging", bufs=4) as staging,
+        tc.psum_pool(name="flip_banks", bufs=4) as flip_banks,
+        tc.psum_pool(name="product_banks", bufs=4) as product_banks,
+    ):
+        rows = []
+        for c in range(S // CHUNK):
+            chunk = held.tile([P, BLOCKS, P], BF16, name=f"rows{c}")
+            source = table[c * CHUNK : (c + 1) * CHUNK, :].rearrange("(b p) k -> p b k", p=P)
+            queue = nc.sync if c % 2 == 0 else nc.scalar
+            queue.dma_start(chunk[:], source)
+            rows.append(chunk)
+        offsets = held.tile([P, N // 16], U16, name="offsets")
+        nc.sync.dma_start(offsets[:], offs)
+        weights = held.tile([P, M], BF16, name="weights")
+        nc.scalar.dma_start(weights[:], w)
+        identity = held.tile([P, P], BF16, name="identity")
+        make_identity(nc, identity[:])
+
+        window = held.tile([P, S], BF16, name="window")
+        for c in range(S // CHUNK):
+            flipped = flip_banks.tile([P, CHUNK], BF16, name="flipped")
+            for b in range(BLOCKS):
+                nc.tensor.transpose(flipped[:, b * P : (b + 1) * P], rows[c][:, b, :], identity[:])
+            if c % 2 == 0:
+                nc.vector.tensor_copy(window[:, c * CHUNK : (c + 1) * CHUNK], flipped[:])
+            else:
+                nc.scalar.copy(window[:, c * CHUNK : (c + 1) * CHUNK], flipped[:])
+
+        for j in range(N // PIECE):
+            looked_up = window[:].indirect(offsets[:, j * (PIECE // 16) : (j + 1) * (PIECE // 16)])
+            for h in range(M // P):
+                product = product_banks.tile([P, PIECE], F32, name="product")
+                nc.tensor.matmul(product[:], weights[:, h * P : (h + 1) * P], looked_up, start=True, stop=True)
+                staged = staging.tile([P, PIECE], F32, name="staged")
+                target = out[h * P : (h + 1) * P, j * PIECE : (j + 1) * PIECE]
+                if h == 0:
+                    nc.vector.tensor_copy(staged[:], product[:])
+                    nc.sync.dma_start(target, staged[:])
+                else:
+                    nc.scalar.copy(staged[:], product[:])
+                    nc.scalar.dma_start(target, staged[:])

@@ -8,7 +8,7 @@ S = 4096
 M = 256
 N = 2048
 PIECE = 512
-BLOCKS = 8
+BLOCKS = 4
 CHUNK = BLOCKS * P
 
 FLOPS = 2 * P * M * N
@@ -25,7 +25,7 @@ def tile_cliffordalgebra_kernel(tc, table, w, offs, out):
         rows = []
         for c in range(S // CHUNK):
             chunk = held.tile([P, BLOCKS, P], BF16, name=f"rows{c}")
-            source = table[c * CHUNK : (c + 1) * CHUNK, :].rearrange("(b p) k -> p b k", p=P)
+            source = table[c * CHUNK : (c + 1) * CHUNK, :].rearrange("(p b) k -> p b k", p=P)
             queue = nc.sync if c % 2 == 0 else nc.scalar
             queue.dma_start(chunk[:], source)
             rows.append(chunk)
@@ -38,13 +38,14 @@ def tile_cliffordalgebra_kernel(tc, table, w, offs, out):
 
         window = held.tile([P, S], BF16, name="window")
         for c in range(S // CHUNK):
-            flipped = flip_banks.tile([P, CHUNK], BF16, name="flipped")
+            flipped = flip_banks.tile([P, BLOCKS, P], BF16, name="flipped")
             for b in range(BLOCKS):
-                nc.tensor.transpose(flipped[:, b * P : (b + 1) * P], rows[c][:, b, :], identity[:])
+                nc.tensor.transpose(flipped[:, b, :], rows[c][:, b, :], identity[:])
+            in_order = window[:, c * CHUNK : (c + 1) * CHUNK].rearrange("k (p b) -> k p b", b=BLOCKS)
             if c % 2 == 0:
-                nc.vector.tensor_copy(window[:, c * CHUNK : (c + 1) * CHUNK], flipped[:])
+                nc.vector.tensor_copy(in_order, flipped[:].rearrange("k b p -> k p b"))
             else:
-                nc.scalar.copy(window[:, c * CHUNK : (c + 1) * CHUNK], flipped[:])
+                nc.scalar.copy(in_order, flipped[:].rearrange("k b p -> k p b"))
 
         for j in range(N // PIECE):
             looked_up = window[:].indirect(offsets[:, j * (PIECE // 16) : (j + 1) * (PIECE // 16)])
@@ -55,7 +56,6 @@ def tile_cliffordalgebra_kernel(tc, table, w, offs, out):
                 target = out[h * P : (h + 1) * P, j * PIECE : (j + 1) * PIECE]
                 if h == 0:
                     nc.vector.tensor_copy(staged[:], product[:])
-                    nc.sync.dma_start(target, staged[:])
                 else:
                     nc.scalar.copy(staged[:], product[:])
-                    nc.scalar.dma_start(target, staged[:])
+                nc.sync.dma_start(target, staged[:])

@@ -10,6 +10,7 @@ N = 2048
 PIECE = 512
 BLOCKS = 4
 CHUNK = BLOCKS * P
+WARM_UPS = 6
 
 FLOPS = 2 * P * M * N
 
@@ -22,6 +23,12 @@ def tile_cliffordalgebra_kernel(tc, table, w, offs, out):
         tc.psum_pool(name="flip_banks", bufs=4) as flip_banks,
         tc.psum_pool(name="product_banks", bufs=4) as product_banks,
     ):
+        zeros = held.tile([P, PIECE], BF16, name="zeros")
+        nc.vector.memset(zeros[:], 0.0)
+        unused = product_banks.tile([P, PIECE], F32, name="product")
+        for i in range(WARM_UPS):
+            nc.tensor.matmul(unused[:], zeros[:, 0:P], zeros[:], start=True, stop=True)
+
         rows = []
         for c in range(S // CHUNK):
             chunk = held.tile([P, BLOCKS, P], BF16, name=f"rows{c}")

@@ -19,7 +19,7 @@ def tile_cliffordalgebra_kernel(tc, table, w, offs, out):
     nc = tc.nc
     with (
         tc.tile_pool(name="held", bufs=1) as held,
-        tc.tile_pool(name="staging", bufs=4) as staging,
+        tc.tile_pool(name="staging", bufs=8) as staging,
         tc.psum_pool(name="flip_banks", bufs=4) as flip_banks,
         tc.psum_pool(name="product_banks", bufs=4) as product_banks,
     ):

@@ -8,18 +8,20 @@ S = 4096
 M = 256
 N = 2048
 PIECE = 512
+PIECES = (PIECE, PIECE, PIECE, PIECE // 2, PIECE // 2)
 BLOCKS = 4
 CHUNK = BLOCKS * P
 WARM_UPS = 6
 
 FLOPS = 2 * P * M * N
+assert sum(PIECES) == N
 
 
 def tile_cliffordalgebra_kernel(tc, table, w, offs, out):
     nc = tc.nc
     with (
         tc.tile_pool(name="held", bufs=1) as held,
-        tc.tile_pool(name="staging", bufs=8) as staging,
+        tc.tile_pool(name="staging", bufs=2 * len(PIECES)) as staging,
         tc.psum_pool(name="flip_banks", bufs=4) as flip_banks,
         tc.psum_pool(name="product_banks", bufs=4) as product_banks,
     ):
@@ -54,15 +56,17 @@ def tile_cliffordalgebra_kernel(tc, table, w, offs, out):
             else:
                 nc.scalar.copy(in_order, flipped[:].rearrange("k b p -> k p b"))
 
-        for j in range(N // PIECE):
-            looked_up = window[:].indirect(offsets[:, j * (PIECE // 16) : (j + 1) * (PIECE // 16)])
+        first = 0
+        for width in PIECES:
+            looked_up = window[:].indirect(offsets[:, first // 16 : (first + width) // 16])
             for h in range(M // P):
-                product = product_banks.tile([P, PIECE], F32, name="product")
+                product = product_banks.tile([P, width], F32, name="product")
                 nc.tensor.matmul(product[:], weights[:, h * P : (h + 1) * P], looked_up, start=True, stop=True)
-                staged = staging.tile([P, PIECE], F32, name="staged")
-                target = out[h * P : (h + 1) * P, j * PIECE : (j + 1) * PIECE]
+                staged = staging.tile([P, width], F32, name="staged")
+                target = out[h * P : (h + 1) * P, first : first + width]
                 if h == 0:
                     nc.vector.tensor_copy(staged[:], product[:])
                 else:
                     nc.scalar.copy(staged[:], product[:])
                 nc.sync.dma_start(target, staged[:])
+            first += width

@@ -8,20 +8,18 @@ S = 4096
 M = 256
 N = 2048
 PIECE = 512
-PIECES = (PIECE, PIECE, PIECE, PIECE // 2, PIECE // 2)
 BLOCKS = 4
 CHUNK = BLOCKS * P
-WARM_UPS = 6
+WARM_UPS = 4
 
 FLOPS = 2 * P * M * N
-assert sum(PIECES) == N
 
 
 def tile_cliffordalgebra_kernel(tc, table, w, offs, out):
     nc = tc.nc
     with (
         tc.tile_pool(name="held", bufs=1) as held,
-        tc.tile_pool(name="staging", bufs=2 * len(PIECES)) as staging,
+        tc.tile_pool(name="staging", bufs=8) as staging,
         tc.psum_pool(name="flip_banks", bufs=4) as flip_banks,
         tc.psum_pool(name="product_banks", bufs=4) as product_banks,
     ):
@@ -56,17 +54,15 @@ def tile_cliffordalgebra_kernel(tc, table, w, offs, out):
             else:
                 nc.scalar.copy(in_order, flipped[:].rearrange("k b p -> k p b"))
 
-        first = 0
-        for width in PIECES:
-            looked_up = window[:].indirect(offsets[:, first // 16 : (first + width) // 16])
+        for j in range(N // PIECE):
+            looked_up = window[:].indirect(offsets[:, j * (PIECE // 16) : (j + 1) * (PIECE // 16)])
             for h in range(M // P):
-                product = product_banks.tile([P, width], F32, name="product")
+                product = product_banks.tile([P, PIECE], F32, name="product")
                 nc.tensor.matmul(product[:], weights[:, h * P : (h + 1) * P], looked_up, start=True, stop=True)
-                staged = staging.tile([P, width], F32, name="staged")
-                target = out[h * P : (h + 1) * P, first : first + width]
+                staged = staging.tile([P, PIECE], F32, name="staged")
+                target = out[h * P : (h + 1) * P, j * PIECE : (j + 1) * PIECE]
                 if h == 0:
                     nc.vector.tensor_copy(staged[:], product[:])
                 else:
                     nc.scalar.copy(staged[:], product[:])
                 nc.sync.dma_start(target, staged[:])
-            first += width

@@ -48,6 +48,7 @@ def tile_cliffordalgebra_kernel(tc, table, w, offs, out):
             flipped = flip_banks.tile([P, BLOCKS, P], BF16, name="flipped")
             for b in range(BLOCKS):
                 nc.tensor.transpose(flipped[:, b, :], rows[c][:, b, :], identity[:])
+            nc.tensor.matmul(unused[:], identity[:], rows[c][:].rearrange("p b k -> p (b k)"), start=True, stop=True)
             in_order = window[:, c * CHUNK : (c + 1) * CHUNK].rearrange("k (p b) -> k p b", b=BLOCKS)
             if c % 2 == 0:
                 nc.vector.tensor_copy(in_order, flipped[:].rearrange("k b p -> k p b"))

@@ -10,7 +10,7 @@ N = 2048
 PIECE = 512
 BLOCKS = 4
 CHUNK = BLOCKS * P
-WARM_UPS = 4
+WARM_UPS = 2
 
 FLOPS = 2 * P * M * N
 
@@ -25,6 +25,8 @@ def tile_cliffordalgebra_kernel(tc, table, w, offs, out):
     ):
         zeros = held.tile([P, PIECE], BF16, name="zeros")
         nc.vector.memset(zeros[:], 0.0)
+        early = held.tile([P, 1], BF16, name="early")
+        nc.scalar.copy(early[:], zeros[:, 0:1])
         unused = product_banks.tile([P, PIECE], F32, name="product")
         for i in range(WARM_UPS):
             nc.tensor.matmul(unused[:], zeros[:, 0:P], zeros[:], start=True, stop=True)
@@ -48,7 +50,8 @@ def tile_cliffordalgebra_kernel(tc, table, w, offs, out):
             flipped = flip_banks.tile([P, BLOCKS, P], BF16, name="flipped")
             for b in range(BLOCKS):
                 nc.tensor.transpose(flipped[:, b, :], rows[c][:, b, :], identity[:])
-            nc.tensor.matmul(unused[:], identity[:], rows[c][:].rearrange("p b k -> p (b k)"), start=True, stop=True)
+            if c % 2 == 1:
+                nc.tensor.matmul(unused[:], identity[:], rows[c][:].rearrange("p b k -> p (b k)"), start=True, stop=True)
             in_order = window[:, c * CHUNK : (c + 1) * CHUNK].rearrange("k (p b) -> k p b", b=BLOCKS)
             if c % 2 == 0:
                 nc.vector.tensor_copy(in_order, flipped[:].rearrange("k b p -> k p b"))

@@ -10,7 +10,7 @@ N = 2048
 PIECE = 512
 BLOCKS = 4
 CHUNK = BLOCKS * P
-WARM_UPS = 2
+WARM_UPS = 4
 
 FLOPS = 2 * P * M * N
 
@@ -24,7 +24,7 @@ def tile_cliffordalgebra_kernel(tc, table, w, offs, out):
         tc.psum_pool(name="product_banks", bufs=4) as product_banks,
     ):
         zeros = held.tile([P, PIECE], BF16, name="zeros")
-        nc.vector.memset(zeros[:], 0.0)
+        nc.gpsimd.memset(zeros[:], 0.0)
         early = held.tile([P, 1], BF16, name="early")
         nc.scalar.copy(early[:], zeros[:, 0:1])
         unused = product_banks.tile([P, PIECE], F32, name="product")

@@ -23,13 +23,14 @@ def tile_cliffordalgebra_kernel(tc, table, w, offs, out):
         tc.psum_pool(name="flip_banks", bufs=4) as flip_banks,
         tc.psum_pool(name="product_banks", bufs=4) as product_banks,
     ):
-        zeros = held.tile([P, PIECE], BF16, name="zeros")
+        zeros = held.tile([P, P], BF16, name="zeros")
         nc.gpsimd.memset(zeros[:], 0.0)
+        zeros_again = zeros[:].unsqueeze(1).to_broadcast([P, PIECE // P, P])
         early = held.tile([P, 1], BF16, name="early")
         nc.scalar.copy(early[:], zeros[:, 0:1])
         unused = product_banks.tile([P, PIECE], F32, name="product")
         for i in range(WARM_UPS):
-            nc.tensor.matmul(unused[:], zeros[:, 0:P], zeros[:], start=True, stop=True)
+            nc.tensor.matmul(unused[:], zeros[:], zeros_again, start=True, stop=True)
 
         rows = []
         for c in range(S // CHUNK):

@@ -10,6 +10,7 @@ N = 2048
 PIECE = 512
 BLOCKS = 4
 CHUNK = BLOCKS * P
+WIDTHS = (256, 256, 512, 512, 256, 256)
 WARM_UPS = 4
 
 FLOPS = 2 * P * M * N
@@ -19,7 +20,7 @@ def tile_cliffordalgebra_kernel(tc, table, w, offs, out):
     nc = tc.nc
     with (
         tc.tile_pool(name="held", bufs=1) as held,
-        tc.tile_pool(name="staging", bufs=8) as staging,
+        tc.tile_pool(name="staging", bufs=12) as staging,
         tc.psum_pool(name="flip_banks", bufs=4) as flip_banks,
         tc.psum_pool(name="product_banks", bufs=4) as product_banks,
     ):
@@ -59,15 +60,17 @@ def tile_cliffordalgebra_kernel(tc, table, w, offs, out):
             else:
                 nc.scalar.copy(in_order, flipped[:].rearrange("k b p -> k p b"))
 
-        for j in range(N // PIECE):
-            looked_up = window[:].indirect(offsets[:, j * (PIECE // 16) : (j + 1) * (PIECE // 16)])
+        first = 0
+        for width in WIDTHS:
+            looked_up = window[:].indirect(offsets[:, first // 16 : (first + width) // 16])
             for h in range(M // P):
                 product = product_banks.tile([P, PIECE], F32, name="product")
-                nc.tensor.matmul(product[:], weights[:, h * P : (h + 1) * P], looked_up, start=True, stop=True)
+                nc.tensor.matmul(product[:, 0:width], weights[:, h * P : (h + 1) * P], looked_up, start=True, stop=True)
                 staged = staging.tile([P, PIECE], F32, name="staged")
-                target = out[h * P : (h + 1) * P, j * PIECE : (j + 1) * PIECE]
+                target = out[h * P : (h + 1) * P, first : first + width]
                 if h == 0:
-                    nc.vector.tensor_copy(staged[:], product[:])
+                    nc.vector.tensor_copy(staged[:, 0:width], product[:, 0:width])
                 else:
-                    nc.scalar.copy(staged[:], product[:])
-                nc.sync.dma_start(target, staged[:])
+                    nc.scalar.copy(staged[:, 0:width], product[:, 0:width])
+                nc.sync.dma_start(target, staged[:, 0:width])
+            first += width

@@ -21,15 +21,15 @@ def tile_cliffordalgebra_kernel(tc, table, w, offs, out):
     with (
         tc.tile_pool(name="held", bufs=1) as held,
         tc.tile_pool(name="staging", bufs=12) as staging,
-        tc.psum_pool(name="flip_banks", bufs=4) as flip_banks,
-        tc.psum_pool(name="product_banks", bufs=4) as product_banks,
+        tc.psum_pool(name="idle_bank", bufs=1) as idle_bank,
+        tc.psum_pool(name="banks", bufs=7) as banks,
     ):
         zeros = held.tile([P, P], BF16, name="zeros")
         nc.gpsimd.memset(zeros[:], 0.0)
         zeros_again = zeros[:].unsqueeze(1).to_broadcast([P, PIECE // P, P])
         early = held.tile([P, 1], BF16, name="early")
         nc.scalar.copy(early[:], zeros[:, 0:1])
-        unused = product_banks.tile([P, PIECE], F32, name="product")
+        unused = idle_bank.tile([P, PIECE], F32, name="unused")
         for i in range(WARM_UPS):
             nc.tensor.matmul(unused[:], zeros[:], zeros_again, start=True, stop=True)
 
@@ -49,7 +49,7 @@ def tile_cliffordalgebra_kernel(tc, table, w, offs, out):
 
         window = held.tile([P, S], BF16, name="window")
         for c in range(S // CHUNK):
-            flipped = flip_banks.tile([P, BLOCKS, P], BF16, name="flipped")
+            flipped = banks.tile([P, BLOCKS, P], BF16, name="flipped", tag="bank")
             for b in range(BLOCKS):
                 nc.tensor.transpose(flipped[:, b, :], rows[c][:, b, :], identity[:])
             if c % 2 == 1:
@@ -64,7 +64,7 @@ def tile_cliffordalgebra_kernel(tc, table, w, offs, out):
         for width in WIDTHS:
             looked_up = window[:].indirect(offsets[:, first // 16 : (first + width) // 16])
             for h in range(M // P):
-                product = product_banks.tile([P, PIECE], F32, name="product")
+                product = banks.tile([P, PIECE], F32, name="product", tag="bank")
                 nc.tensor.matmul(product[:, 0:width], weights[:, h * P : (h + 1) * P], looked_up, start=True, stop=True)
                 staged = staging.tile([P, PIECE], F32, name="staged")
                 target = out[h * P : (h + 1) * P, first : first + width]

@@ -27,8 +27,6 @@ def tile_cliffordalgebra_kernel(tc, table, w, offs, out):
         zeros = held.tile([P, P], BF16, name="zeros")
         nc.gpsimd.memset(zeros[:], 0.0)
         zeros_again = zeros[:].unsqueeze(1).to_broadcast([P, PIECE // P, P])
-        early = held.tile([P, 1], BF16, name="early")
-        nc.scalar.copy(early[:], zeros[:, 0:1])
         unused = idle_bank.tile([P, PIECE], F32, name="unused")
         for i in range(WARM_UPS):
             nc.tensor.matmul(unused[:], zeros[:], zeros_again, start=True, stop=True)
@@ -40,10 +38,12 @@ def tile_cliffordalgebra_kernel(tc, table, w, offs, out):
             queue = nc.sync if c % 2 == 0 else nc.scalar
             queue.dma_start(chunk[:], source)
             rows.append(chunk)
+        early = held.tile([P, 1], BF16, name="early")
+        nc.scalar.copy(early[:], zeros[:, 0:1])
         offsets = held.tile([P, N // 16], U16, name="offsets")
         nc.sync.dma_start(offsets[:], offs)
         weights = held.tile([P, M], BF16, name="weights")
-        nc.scalar.dma_start(weights[:], w)
+        nc.sync.dma_start(weights[:], w)
         identity = held.tile([P, P], BF16, name="identity")
         make_identity(nc, identity[:])
 

@@ -10,7 +10,7 @@ N = 2048
 PIECE = 512
 BLOCKS = 4
 CHUNK = BLOCKS * P
-WIDTHS = (256, 256, 512, 512, 256, 256)
+WIDTHS = (256, 384, 512, 512, 384)
 WARM_UPS = 4
 
 FLOPS = 2 * P * M * N
@@ -72,5 +72,7 @@ def tile_cliffordalgebra_kernel(tc, table, w, offs, out):
                     nc.vector.tensor_copy(staged[:, 0:width], product[:, 0:width])
                 else:
                     nc.scalar.copy(staged[:, 0:width], product[:, 0:width])
-                nc.sync.dma_start(target, staged[:, 0:width])
+                last = h == 1 and first + width == N
+                queue = nc.scalar if last else nc.sync
+                queue.dma_start(target, staged[:, 0:width])
             first += width

import concourse.mybir as mybir
from concourse.masks import make_identity

BF16, F32, U16 = mybir.dt.bfloat16, mybir.dt.float32, mybir.dt.uint16

P = 128
S = 4096
M = 256
N = 2048
PIECE = 512
BLOCKS = 4
CHUNK = BLOCKS * P
WIDTHS = (256, 384, 512, 512, 384)
WARM_UPS = 4

FLOPS = 2 * P * M * N


def tile_cliffordalgebra_kernel(tc, table, w, offs, out):
    nc = tc.nc
    with (
        tc.tile_pool(name="held", bufs=1) as held,
        tc.tile_pool(name="staging", bufs=12) as staging,
        tc.psum_pool(name="idle_bank", bufs=1) as idle_bank,
        tc.psum_pool(name="banks", bufs=7) as banks,
    ):
        zeros = held.tile([P, P], BF16, name="zeros")
        nc.gpsimd.memset(zeros[:], 0.0)
        zeros_again = zeros[:].unsqueeze(1).to_broadcast([P, PIECE // P, P])
        unused = idle_bank.tile([P, PIECE], F32, name="unused")
        for i in range(WARM_UPS):
            nc.tensor.matmul(unused[:], zeros[:], zeros_again, start=True, stop=True)

        rows = []
        for c in range(S // CHUNK):
            chunk = held.tile([P, BLOCKS, P], BF16, name=f"rows{c}")
            source = table[c * CHUNK : (c + 1) * CHUNK, :].rearrange("(p b) k -> p b k", p=P)
            queue = nc.sync if c % 2 == 0 else nc.scalar
            queue.dma_start(chunk[:], source)
            rows.append(chunk)
        early = held.tile([P, 1], BF16, name="early")
        nc.scalar.copy(early[:], zeros[:, 0:1])
        offsets = held.tile([P, N // 16], U16, name="offsets")
        nc.sync.dma_start(offsets[:], offs)
        weights = held.tile([P, M], BF16, name="weights")
        nc.sync.dma_start(weights[:], w)
        identity = held.tile([P, P], BF16, name="identity")
        make_identity(nc, identity[:])

        window = held.tile([P, S], BF16, name="window")
        for c in range(S // CHUNK):
            flipped = banks.tile([P, BLOCKS, P], BF16, name="flipped", tag="bank")
            for b in range(BLOCKS):
                nc.tensor.transpose(flipped[:, b, :], rows[c][:, b, :], identity[:])
            if c % 2 == 1:
                nc.tensor.matmul(unused[:], identity[:], rows[c][:].rearrange("p b k -> p (b k)"), start=True, stop=True)
            in_order = window[:, c * CHUNK : (c + 1) * CHUNK].rearrange("k (p b) -> k p b", b=BLOCKS)
            if c % 2 == 0:
                nc.vector.tensor_copy(in_order, flipped[:].rearrange("k b p -> k p b"))
            else:
                nc.scalar.copy(in_order, flipped[:].rearrange("k b p -> k p b"))

        first = 0
        for width in WIDTHS:
            looked_up = window[:].indirect(offsets[:, first // 16 : (first + width) // 16])
            for h in range(M // P):
                product = banks.tile([P, PIECE], F32, name="product", tag="bank")
                nc.tensor.matmul(product[:, 0:width], weights[:, h * P : (h + 1) * P], looked_up, start=True, stop=True)
                staged = staging.tile([P, PIECE], F32, name="staged")
                target = out[h * P : (h + 1) * P, first : first + width]
                if h == 0:
                    nc.vector.tensor_copy(staged[:, 0:width], product[:, 0:width])
                else:
                    nc.scalar.copy(staged[:, 0:width], product[:, 0:width])
                last = h == 1 and first + width == N
                queue = nc.scalar if last else nc.sync
                queue.dma_start(target, staged[:, 0:width])
            first += width
